import numpy as np
import ml_dtypes


def mxq(x, axis, fmt="e4m3"):
    dtype, down = {"e4m3": (ml_dtypes.float8_e4m3fn, 7), "e5m2": (ml_dtypes.float8_e5m2, 14)}[fmt]
    v = np.moveaxis(np.asarray(x, np.float32).astype(ml_dtypes.bfloat16).astype(np.float64), axis, -1)
    blocks = v.reshape(v.shape[:-1] + (-1, 32))
    amax = np.abs(blocks).max(-1, keepdims=True)
    byte = np.maximum(np.where(amax > 0, np.frexp(amax)[1] - 1 + 127, 0) - down, 1)
    scale = np.exp2(byte - 127.0)
    codes = (blocks / scale).astype(np.float32).astype(dtype).astype(np.float64)
    return np.moveaxis((codes * scale).reshape(v.shape), -1, axis)


WIDE = False


def mx_kscale(k):
    if not WIDE:
        return np.ones(k)
    levels = np.array([10, -10, 5, -5, 0])
    if k % 512:
        return np.exp2(np.random.permutation(np.resize(levels, k // 32))).repeat(32)
    a = np.empty((k // 512, 16))
    for p in range(k // 512):
        a[p, :8] = np.random.permutation(np.resize(levels, 8))
        for g in range(8):
            far = levels[np.abs(levels - a[p, g]) >= 10]
            a[p, g + 8] = far[np.random.randint(len(far))]
    return np.exp2(a.ravel()).repeat(32)


BF16 = ml_dtypes.bfloat16


def bf(x):
    return np.asarray(x, np.float32).astype(BF16)


def f64(x):
    return np.asarray(x).astype(np.float64)


B, I, H = 4096, 512, 512
EPS = 1e-5


def sigmoid(v):
    return 1.0 / (1.0 + np.exp(-v))


def ln(v, g, b):
    m = v.mean(-1, keepdims=True)
    var = np.square(v - m).mean(-1, keepdims=True)
    return (v - m) / np.sqrt(var + EPS) * g + b


def setup_inputs():
    s, t = mx_kscale(I), mx_kscale(H)
    d = {"x": bf(np.random.standard_normal((B, I)) * s), "h": bf(np.random.standard_normal((B, H)) * t),
         "c": bf(np.random.standard_normal((B, H))), "ic_tilde": bf(0.35 * np.random.standard_normal((B, H)))}
    for g in ("f", "o"):
        d["W" + g + "_w"] = bf(np.random.standard_normal((H, I)) / np.sqrt(I) / s[None, :])
        d["W" + g + "_b"] = bf(np.random.standard_normal(H) * 0.5)
        d["U" + g + "_w"] = bf(np.random.standard_normal((H, H)) / np.sqrt(H) / t[None, :])
        d["ln" + g + "_g"] = bf(1.0 + 0.2 * np.random.standard_normal(H))
        d["ln" + g + "_b"] = bf(0.2 * np.random.standard_normal(H))
    return d


def reference(x, h, c, ic_tilde, Wf_w, Wf_b, Uf_w, lnf_g, lnf_b, Wo_w, Wo_b, Uo_w, lno_g, lno_b):
    xq = mxq(f64(x), 1, "e4m3")
    hq = mxq(f64(h), 1, "e4m3")
    pre_f = (xq @ mxq(f64(Wf_w), 1, "e4m3").T) + f64(Wf_b) + (hq @ mxq(f64(Uf_w), 1, "e4m3").T)
    pre_o = (xq @ mxq(f64(Wo_w), 1, "e4m3").T) + f64(Wo_b) + (hq @ mxq(f64(Uo_w), 1, "e4m3").T)
    f = sigmoid(ln(pre_f, f64(lnf_g), f64(lnf_b)))
    o = sigmoid(ln(pre_o, f64(lno_g), f64(lno_b)))
    c_new = f * f64(c) + f64(ic_tilde)
    h_new = o * np.tanh(c_new)
    return (h_new, c_new)

@@ -1,0 +1,296 @@
+from contextlib import ExitStack
+
+import concourse.mybir as mybir
+from concourse.masks import make_identity
+
+F32 = mybir.dt.float32
+BF16 = mybir.dt.bfloat16
+U32 = mybir.dt.uint32
+U8 = mybir.dt.uint8
+FP8X4 = mybir.dt.float8_e4m3fn_x4
+ALU = mybir.AluOpType
+ACT = mybir.ActivationFunctionType
+
+P = 128
+BATCH = 4096
+K = 512
+FEAT = 512
+WORDS = K // 2
+TILES = 2
+GROUPS = BATCH // (P * TILES)
+GATES = 2
+EPS = 1e-5
+VECTOR_EVERY = 4
+
+FLOPS = 4 * 2 * BATCH * K * FEAT
+
+
+def tile_layernormlstmcell_pb_t_kernel(
+    tc, x, h, c, ic_tilde, Wf_w, Wf_b, Uf_w, lnf_g, lnf_b, Wo_w, Wo_b, Uo_w, lno_g, lno_b, out_0, out_1
+):
+    nc = tc.nc
+    with ExitStack() as ctx:
+        ctx.enter_context(tc.manual_schedule())
+        consts = ctx.enter_context(tc.tile_pool(name="consts", bufs=1))
+        wstage = ctx.enter_context(tc.tile_pool(name="wstage", bufs=2))
+        loads = ctx.enter_context(tc.tile_pool(name="loads", bufs=4))
+        mxin = ctx.enter_context(tc.tile_pool(name="mxin", bufs=2))
+        stats = ctx.enter_context(tc.tile_pool(name="stats", bufs=3))
+        acts = ctx.enter_context(tc.tile_pool(name="acts", bufs=5))
+        psum_keep = ctx.enter_context(tc.psum_pool(name="psum_keep", bufs=1))
+        psum = ctx.enter_context(tc.psum_pool(name="psum", bufs=2))
+
+        ident = consts.tile([P, P], F32)
+        make_identity(nc, ident[:])
+        ones = consts.tile([P, P], BF16)
+        nc.vector.memset(ones[:], 1.0)
+        neg_half = consts.tile([P, TILES * GATES], F32)
+        nc.vector.memset(neg_half[:], -0.5)
+        vec_rows = consts.tile([P, 6 * FEAT], BF16)
+        nc.vector.memset(vec_rows[:], 0.0)
+        warm = consts.tile([P, 1], F32)
+        nc.scalar.activation(out=warm[:], in_=neg_half[:, 0:1], func=ACT.Sigmoid)
+
+        w_codes = consts.tile([P, 4 * FEAT], U32, align_bytes=64)
+        w_scales = consts.tile([P, 4 * FEAT], U8, align_bytes=64)
+        raws = []
+        for w, weight in enumerate((Wf_w, Uf_w, Wo_w, Uo_w)):
+            raw = consts.tile([P, 4 * K], BF16, name="raw%d" % w)
+            nc.sync.dma_start(
+                out=raw[:].rearrange("p (b k) -> p b k", b=4),
+                in_=weight.rearrange("(b p) k -> p b k", p=P),
+            )
+            raws.append(raw)
+        for v, vec in enumerate((Wf_b, Wo_b, lnf_g, lnf_b, lno_g, lno_b)):
+            nc.sync.dma_start(out=vec_rows[0:1, v * FEAT : (v + 1) * FEAT], in_=vec.unsqueeze(0))
+        for w in range(4):
+            raw_words = raws[w][:].bitcast(F32)
+            grouped = wstage.tile([P, 4 * FEAT], BF16, align_bytes=64)
+            grouped_words = grouped[:].bitcast(F32).rearrange("p (j u) -> p j u", u=2)
+            for half in range(2):
+                turned = psum.tile([P, 2, 2 * P], F32, tag="turned")
+                for u in range(2):
+                    for b in range(2):
+                        first = (2 * half + b) * WORDS
+                        nc.tensor.transpose(
+                            out=turned[:, u, b * P : (b + 1) * P],
+                            in_=raw_words[:, first + u : first + WORDS : 2],
+                            identity=ident[:],
+                        )
+                copy = nc.scalar.copy if half == 0 else nc.vector.tensor_copy
+                copy(
+                    out=grouped_words[:, half * 2 * P : (half + 1) * 2 * P, :],
+                    in_=turned[:].rearrange("p u j -> p j u"),
+                )
+            nc.vector.quantize_mx(
+                out=w_codes[:, w * FEAT : (w + 1) * FEAT].bitcast(FP8X4),
+                scales=w_scales[:, w * FEAT : (w + 1) * FEAT],
+                in_=grouped[:],
+            )
+
+
+        def spread(dest, v):
+            nc.tensor.matmul(
+                out=dest, lhsT=ones[:], rhs=vec_rows[:, v * FEAT : (v + 1) * FEAT], start=True, stop=True
+            )
+
+        bias_ps = psum.tile([P, GATES * FEAT], BF16, tag="acc0")
+        bias = consts.tile([P, GATES * FEAT], BF16)
+        for gate in range(GATES):
+            spread(bias_ps[:, gate * FEAT : (gate + 1) * FEAT], gate)
+        nc.vector.tensor_copy(out=bias[:], in_=bias_ps[:])
+        gain_shift = []
+        for gate in range(GATES):
+            bank = psum_keep.tile([P, 2 * FEAT], BF16, name="gain_shift%d" % gate)
+            spread(bank[:, 0:FEAT], 2 + 2 * gate)
+            spread(bank[:, FEAT : 2 * FEAT], 3 + 2 * gate)
+            gain_shift.append(bank)
+
+        rows = "(g p t) k -> g p (t k)"
+        x_rows = x.rearrange(rows, p=P, t=TILES)
+        h_rows = h.rearrange(rows, p=P, t=TILES)
+        c_rows = c.rearrange(rows, p=P, t=TILES)
+        ic_rows = ic_tilde.rearrange(rows, p=P, t=TILES)
+        h_new_rows = out_0.rearrange(rows, p=P, t=TILES)
+        c_new_rows = out_1.rearrange(rows, p=P, t=TILES)
+        live = {}
+
+        def load_operands(g):
+            xh = loads.tile([P, 2 * TILES * K], BF16, name="xh")
+            nc.sync.dma_start(out=xh[:, 0 : TILES * K], in_=x_rows[g])
+            nc.sync.dma_start(out=xh[:, TILES * K : 2 * TILES * K], in_=h_rows[g])
+            live["xh", g] = xh
+
+        def load_cell(g):
+            c_old = loads.tile([P, TILES * FEAT], BF16, name="c_old")
+            ic = loads.tile([P, TILES * FEAT], BF16, name="ic")
+            nc.sync.dma_start(out=c_old[:], in_=c_rows[g])
+            nc.sync.dma_start(out=ic[:], in_=ic_rows[g])
+            live["c_old", g] = c_old
+            live["ic", g] = ic
+
+        def transpose_operands(g):
+            words = live["xh", g][:].bitcast(F32)
+            for t in range(TILES):
+                turned = psum.tile([P, 4, P], F32, tag="turned")
+                for operand in range(2):
+                    for u in range(2):
+                        first = (operand * TILES + t) * WORDS
+                        nc.tensor.transpose(
+                            out=turned[:, 2 * operand + u, :],
+                            in_=words[:, first + u : first + WORDS : 2],
+                            identity=ident[:],
+                        )
+                live["turned", g, t] = turned
+
+        def regroup_operands(g):
+            grouped = mxin.tile([P, TILES * 2 * P * 4], BF16, name="grouped", align_bytes=64)
+            grouped_words = grouped[:].bitcast(F32).rearrange(
+                "p (t o r u) -> p t o r u", t=TILES, o=2, u=2
+            )
+            for t in range(TILES):
+                nc.scalar.copy(
+                    out=grouped_words[:, t],
+                    in_=live["turned", g, t][:].rearrange("p (o u) r -> p o r u", o=2),
+                )
+            live["grouped", g] = grouped
+
+        def quantise_operands(g):
+            codes = mxin.tile([P, TILES * 2 * P], U32, name="codes", align_bytes=64)
+            scales = mxin.tile([P, TILES * 2 * P], U8, name="scales", align_bytes=64)
+            nc.vector.quantize_mx(out=codes[:].bitcast(FP8X4), scales=scales[:], in_=live["grouped", g][:])
+            live["codes", g] = codes
+            live["scales", g] = scales
+
+        def multiply(g):
+            codes, scales = live["codes", g], live["scales", g]
+            for t in range(TILES):
+                acc = [psum.tile([P, FEAT], F32, name="acc%d" % gate, tag="acc%d" % gate) for gate in range(GATES)]
+                for operand in range(2):
+                    r_cols = slice((2 * t + operand) * P, (2 * t + operand + 1) * P)
+                    for gate in range(GATES):
+                        w_cols = slice((2 * gate + operand) * FEAT, (2 * gate + operand + 1) * FEAT)
+                        nc.tensor.matmul_mx(
+                            out=acc[gate][:],
+                            lhsT=codes[:, r_cols].bitcast(FP8X4),
+                            lhsT_scale=scales[:, r_cols],
+                            rhs=w_codes[:, w_cols].bitcast(FP8X4),
+                            rhs_scale=w_scales[:, w_cols],
+                            start=(operand == 0),
+                            stop=(operand == 1),
+                        )
+                live["acc", g, t] = acc
+
+        def add_bias(g):
+            act = [acts.tile([P, TILES, FEAT], F32, name="act%d" % gate, tag="act%d" % gate) for gate in range(GATES)]
+            sums = stats.tile([P, TILES * GATES], F32, name="sums")
+            for t in range(TILES):
+                for gate in range(GATES):
+                    col = GATES * t + gate
+                    nc.vector.scalar_tensor_tensor(
+                        out=act[gate][:, t, :],
+                        in0=live["acc", g, t][gate][:],
+                        scalar=1.0,
+                        in1=bias[:, gate * FEAT : (gate + 1) * FEAT],
+                        op0=ALU.mult,
+                        op1=ALU.add,
+                        accum_out=sums[:, col : col + 1],
+                    )
+            live["act", g] = act
+            live["sums", g] = sums
+
+        def deviations(g):
+            act = live["act", g]
+            sq_dev = stats.tile([P, TILES * GATES], F32, name="sq_dev")
+            for t in range(TILES):
+                for gate in range(GATES):
+                    col = GATES * t + gate
+                    squares = acts.tile([P, FEAT], F32, name="squares")
+                    nc.scalar.activation(
+                        out=squares[:],
+                        in_=act[gate][:, t, :],
+                        func=ACT.Square,
+                        bias=live["sums", g][:, col : col + 1],
+                        scale=-1.0 * FEAT,
+                        accum_out=sq_dev[:, col : col + 1],
+                    )
+            neg_mean = stats.tile([P, TILES * GATES], F32, name="neg_mean")
+            nc.scalar.mul(out=neg_mean[:], in_=live["sums", g][:], mul=-1.0 / FEAT)
+            live["neg_mean", g] = neg_mean
+            live["sq_dev", g] = sq_dev
+
+        def centre_and_gain(g):
+            for t in range(TILES):
+                for gate in range(GATES):
+                    col = GATES * t + gate
+                    nc.vector.scalar_tensor_tensor(
+                        out=live["act", g][gate][:, t, :],
+                        in0=live["act", g][gate][:, t, :],
+                        scalar=live["neg_mean", g][:, col : col + 1],
+                        in1=gain_shift[gate][:, 0:FEAT],
+                        op0=ALU.add,
+                        op1=ALU.mult,
+                    )
+
+        def inverse_std(g):
+            var_eps = stats.tile([P, TILES * GATES], F32, name="var_eps")
+            rstd = stats.tile([P, TILES * GATES], F32, name="rstd")
+            nc.gpsimd.tensor_scalar(
+                out=var_eps[:], in0=live["sq_dev", g][:], scalar1=1.0 / FEAT**3, scalar2=EPS, op0=ALU.mult, op1=ALU.add
+            )
+            nc.gpsimd.tensor_tensor(out=rstd[:], in0=var_eps[:], in1=neg_half[:], op=ALU.pow)
+            live["rstd", g] = rstd
+
+        def scale_and_shift(g):
+            for gate in range(GATES):
+                for t in range(TILES):
+                    col = GATES * t + gate
+                    nc.vector.scalar_tensor_tensor(
+                        out=live["act", g][gate][:, t, :],
+                        in0=live["act", g][gate][:, t, :],
+                        scalar=live["rstd", g][:, col : col + 1],
+                        in1=gain_shift[gate][:, FEAT : 2 * FEAT],
+                        op0=ALU.mult,
+                        op1=ALU.add,
+                    )
+
+        def sigmoids(g):
+            for gate in range(GATES):
+                nc.scalar.activation(out=live["act", g][gate][:], in_=live["act", g][gate][:], func=ACT.Sigmoid)
+
+        def updater(g):
+            return nc.vector if (GROUPS - 1 - g) % VECTOR_EVERY == 0 else nc.gpsimd
+
+        def new_cell(g):
+            cell = live["act", g][0][:].rearrange("p t f -> p (t f)")
+            updater(g).tensor_tensor(out=cell, in0=cell, in1=live["c_old", g][:], op=ALU.mult)
+            updater(g).tensor_tensor(out=cell, in0=cell, in1=live["ic", g][:], op=ALU.add)
+            tanh_c = acts.tile([P, TILES * FEAT], F32, name="tanh_c")
+            nc.scalar.activation(out=tanh_c[:], in_=cell, func=ACT.Tanh)
+            nc.sync.dma_start(out=c_new_rows[g], in_=cell)
+            live["tanh_c", g] = tanh_c
+
+        def new_hidden(g):
+            hidden = live["act", g][1][:].rearrange("p t f -> p (t f)")
+            updater(g).tensor_tensor(out=hidden, in0=hidden, in1=live["tanh_c", g][:], op=ALU.mult)
+            nc.sync.dma_start(out=h_new_rows[g], in_=hidden)
+
+        def at(stage, g):
+            if 0 <= g < GROUPS:
+                stage(g)
+
+        for step in range(-3, GROUPS + 3):
+            at(load_operands, step + 3)
+            at(load_cell, step)
+            at(regroup_operands, step + 1)
+            at(transpose_operands, step + 2)
+            at(add_bias, step)
+            at(deviations, step)
+            at(quantise_operands, step + 1)
+            at(multiply, step + 1)
+            at(scale_and_shift, step - 1)
+            at(sigmoids, step - 1)
+            at(centre_and_gain, step)
+            at(new_cell, step - 2)
+            at(inverse_std, step)
+            at(new_hidden, step - 3)

@@ -15,12 +15,12 @@ P = 128
 BATCH = 4096
 K = 512
 FEAT = 512
+BLOCKS = FEAT // P
 WORDS = K // 2
 TILES = 2
 GROUPS = BATCH // (P * TILES)
 GATES = 2
 EPS = 1e-5
-VECTOR_EVERY = 4
 
 FLOPS = 4 * 2 * BATCH * K * FEAT
 
@@ -34,20 +34,23 @@ def tile_layernormlstmcell_pb_t_kernel(
         consts = ctx.enter_context(tc.tile_pool(name="consts", bufs=1))
         wstage = ctx.enter_context(tc.tile_pool(name="wstage", bufs=2))
         loads = ctx.enter_context(tc.tile_pool(name="loads", bufs=4))
-        mxin = ctx.enter_context(tc.tile_pool(name="mxin", bufs=2))
-        stats = ctx.enter_context(tc.tile_pool(name="stats", bufs=3))
-        acts = ctx.enter_context(tc.tile_pool(name="acts", bufs=5))
-        psum_keep = ctx.enter_context(tc.psum_pool(name="psum_keep", bufs=1))
+        mxin = ctx.enter_context(tc.tile_pool(name="mxin", bufs=3))
+        stats = ctx.enter_context(tc.tile_pool(name="stats", bufs=4))
+        acts = ctx.enter_context(tc.tile_pool(name="acts", bufs=4))
         psum = ctx.enter_context(tc.psum_pool(name="psum", bufs=2))
 
         ident = consts.tile([P, P], F32)
         make_identity(nc, ident[:])
+        ident_bf16 = consts.tile([P, P], BF16)
+        nc.vector.tensor_copy(out=ident_bf16[:], in_=ident[:])
         ones = consts.tile([P, P], BF16)
         nc.vector.memset(ones[:], 1.0)
         neg_half = consts.tile([P, TILES * GATES], F32)
         nc.vector.memset(neg_half[:], -0.5)
-        vec_rows = consts.tile([P, 6 * FEAT], BF16)
-        nc.vector.memset(vec_rows[:], 0.0)
+        bias_rows = consts.tile([P, GATES * FEAT], BF16)
+        nc.vector.memset(bias_rows[:], 0.0)
+        affine_rows = consts.tile([P, P], BF16)
+        nc.vector.memset(affine_rows[:], 0.0)
         warm = consts.tile([P, 1], F32)
         nc.scalar.activation(out=warm[:], in_=neg_half[:, 0:1], func=ACT.Sigmoid)
 
@@ -61,8 +64,12 @@ def tile_layernormlstmcell_pb_t_kernel(
                 in_=weight.rearrange("(b p) k -> p b k", p=P),
             )
             raws.append(raw)
-        for v, vec in enumerate((Wf_b, Wo_b, lnf_g, lnf_b, lno_g, lno_b)):
-            nc.sync.dma_start(out=vec_rows[0:1, v * FEAT : (v + 1) * FEAT], in_=vec.unsqueeze(0))
+        for v, vec in enumerate((Wf_b, Wo_b)):
+            nc.sync.dma_start(out=bias_rows[0:1, v * FEAT : (v + 1) * FEAT], in_=vec.unsqueeze(0))
+        for v, vec in enumerate((lnf_g, lnf_b, lno_g, lno_b)):
+            nc.sync.dma_start(
+                out=affine_rows[BLOCKS * v : BLOCKS * (v + 1), :], in_=vec.rearrange("(j p) -> j p", p=P)
+            )
         for w in range(4):
             raw_words = raws[w][:].bitcast(F32)
             grouped = wstage.tile([P, 4 * FEAT], BF16, align_bytes=64)
@@ -88,23 +95,16 @@ def tile_layernormlstmcell_pb_t_kernel(
                 in_=grouped[:],
             )
 
-
-        def spread(dest, v):
-            nc.tensor.matmul(
-                out=dest, lhsT=ones[:], rhs=vec_rows[:, v * FEAT : (v + 1) * FEAT], start=True, stop=True
-            )
-
-        bias_ps = psum.tile([P, GATES * FEAT], BF16, tag="acc0")
+        bias_ps = psum.tile([P, GATES * FEAT], BF16, name="bias_ps", tag="acc")
         bias = consts.tile([P, GATES * FEAT], BF16)
         for gate in range(GATES):
-            spread(bias_ps[:, gate * FEAT : (gate + 1) * FEAT], gate)
+            cols = slice(gate * FEAT, (gate + 1) * FEAT)
+            nc.tensor.matmul(out=bias_ps[:, cols], lhsT=ones[:], rhs=bias_rows[:, cols], start=True, stop=True)
         nc.vector.tensor_copy(out=bias[:], in_=bias_ps[:])
-        gain_shift = []
-        for gate in range(GATES):
-            bank = psum_keep.tile([P, 2 * FEAT], BF16, name="gain_shift%d" % gate)
-            spread(bank[:, 0:FEAT], 2 + 2 * gate)
-            spread(bank[:, FEAT : 2 * FEAT], 3 + 2 * gate)
-            gain_shift.append(bank)
+        affine_ps = psum.tile([P, GATES * FEAT], BF16, name="affine_ps", tag="back")
+        nc.tensor.transpose(out=affine_ps[:, 0:P], in_=affine_rows[:], identity=ident_bf16[:])
+        affine = consts.tile([P, 4 * BLOCKS], F32)
+        nc.vector.tensor_copy(out=affine[:], in_=affine_ps[:, 0 : 4 * BLOCKS])
 
         rows = "(g p t) k -> g p (t k)"
         x_rows = x.rearrange(rows, p=P, t=TILES)
@@ -122,38 +122,31 @@ def tile_layernormlstmcell_pb_t_kernel(
             live["xh", g] = xh
 
         def load_cell(g):
-            c_old = loads.tile([P, TILES * FEAT], BF16, name="c_old")
-            ic = loads.tile([P, TILES * FEAT], BF16, name="ic")
-            nc.sync.dma_start(out=c_old[:], in_=c_rows[g])
-            nc.sync.dma_start(out=ic[:], in_=ic_rows[g])
+            c_old = loads.tile([P, TILES, FEAT], BF16, name="c_old")
+            ic = loads.tile([P, TILES, FEAT], BF16, name="ic")
+            nc.sync.dma_start(out=c_old[:].rearrange("p t f -> p (t f)"), in_=c_rows[g])
+            nc.sync.dma_start(out=ic[:].rearrange("p t f -> p (t f)"), in_=ic_rows[g])
             live["c_old", g] = c_old
             live["ic", g] = ic
 
-        def transpose_operands(g):
+        def transpose_operands(g, t):
             words = live["xh", g][:].bitcast(F32)
-            for t in range(TILES):
-                turned = psum.tile([P, 4, P], F32, tag="turned")
-                for operand in range(2):
-                    for u in range(2):
-                        first = (operand * TILES + t) * WORDS
-                        nc.tensor.transpose(
-                            out=turned[:, 2 * operand + u, :],
-                            in_=words[:, first + u : first + WORDS : 2],
-                            identity=ident[:],
-                        )
-                live["turned", g, t] = turned
-
-        def regroup_operands(g):
-            grouped = mxin.tile([P, TILES * 2 * P * 4], BF16, name="grouped", align_bytes=64)
-            grouped_words = grouped[:].bitcast(F32).rearrange(
+            turned = psum.tile([P, 4, P], F32, name="turned", tag="turned")
+            for operand in range(2):
+                for u in range(2):
+                    first = (operand * TILES + t) * WORDS
+                    nc.tensor.transpose(
+                        out=turned[:, 2 * operand + u, :],
+                        in_=words[:, first + u : first + WORDS : 2],
+                        identity=ident[:],
+                    )
+            if t == 0:
+                live["grouped", g] = mxin.tile([P, TILES * 2 * P * 4], BF16, name="grouped", align_bytes=64)
+            grouped_words = live["grouped", g][:].bitcast(F32).rearrange(
                 "p (t o r u) -> p t o r u", t=TILES, o=2, u=2
             )
-            for t in range(TILES):
-                nc.scalar.copy(
-                    out=grouped_words[:, t],
-                    in_=live["turned", g, t][:].rearrange("p (o u) r -> p o r u", o=2),
-                )
-            live["grouped", g] = grouped
+            copy = nc.scalar.copy if t == 0 else nc.vector.tensor_copy
+            copy(out=grouped_words[:, t], in_=turned[:].rearrange("p (o u) r -> p o r u", o=2))
 
         def quantise_operands(g):
             codes = mxin.tile([P, TILES * 2 * P], U32, name="codes", align_bytes=64)
@@ -162,135 +155,151 @@ def tile_layernormlstmcell_pb_t_kernel(
             live["codes", g] = codes
             live["scales", g] = scales
 
-        def multiply(g):
+        def multiply(g, t):
             codes, scales = live["codes", g], live["scales", g]
-            for t in range(TILES):
-                acc = [psum.tile([P, FEAT], F32, name="acc%d" % gate, tag="acc%d" % gate) for gate in range(GATES)]
+            if t == 0:
+                live["act", g] = acts.tile([P, GATES, TILES, FEAT], F32, name="act")
+                live["sums", g] = stats.tile([P, TILES * GATES], F32, name="sums")
+            for gate in range(GATES):
+                acc = psum.tile([P, FEAT], F32, name="acc", tag="acc")
                 for operand in range(2):
                     r_cols = slice((2 * t + operand) * P, (2 * t + operand + 1) * P)
-                    for gate in range(GATES):
-                        w_cols = slice((2 * gate + operand) * FEAT, (2 * gate + operand + 1) * FEAT)
-                        nc.tensor.matmul_mx(
-                            out=acc[gate][:],
-                            lhsT=codes[:, r_cols].bitcast(FP8X4),
-                            lhsT_scale=scales[:, r_cols],
-                            rhs=w_codes[:, w_cols].bitcast(FP8X4),
-                            rhs_scale=w_scales[:, w_cols],
-                            start=(operand == 0),
-                            stop=(operand == 1),
-                        )
-                live["acc", g, t] = acc
-
-        def add_bias(g):
-            act = [acts.tile([P, TILES, FEAT], F32, name="act%d" % gate, tag="act%d" % gate) for gate in range(GATES)]
-            sums = stats.tile([P, TILES * GATES], F32, name="sums")
-            for t in range(TILES):
-                for gate in range(GATES):
-                    col = GATES * t + gate
-                    nc.vector.scalar_tensor_tensor(
-                        out=act[gate][:, t, :],
-                        in0=live["acc", g, t][gate][:],
-                        scalar=1.0,
-                        in1=bias[:, gate * FEAT : (gate + 1) * FEAT],
-                        op0=ALU.mult,
-                        op1=ALU.add,
-                        accum_out=sums[:, col : col + 1],
+                    w_cols = slice((2 * gate + operand) * FEAT, (2 * gate + operand + 1) * FEAT)
+                    nc.tensor.matmul_mx(
+                        out=acc[:],
+                        lhsT=codes[:, r_cols].bitcast(FP8X4),
+                        lhsT_scale=scales[:, r_cols],
+                        rhs=w_codes[:, w_cols].bitcast(FP8X4),
+                        rhs_scale=w_scales[:, w_cols],
+                        start=(operand == 0),
+                        stop=(operand == 1),
                     )
-            live["act", g] = act
-            live["sums", g] = sums
+                col = GATES * t + gate
+                nc.vector.scalar_tensor_tensor(
+                    out=live["act", g][:, gate, t, :],
+                    in0=acc[:],
+                    scalar=1.0,
+                    in1=bias[:, gate * FEAT : (gate + 1) * FEAT],
+                    op0=ALU.mult,
+                    op1=ALU.add,
+                    accum_out=live["sums", g][:, col : col + 1],
+                )
 
-        def deviations(g):
-            act = live["act", g]
-            sq_dev = stats.tile([P, TILES * GATES], F32, name="sq_dev")
-            for t in range(TILES):
-                for gate in range(GATES):
-                    col = GATES * t + gate
-                    squares = acts.tile([P, FEAT], F32, name="squares")
-                    nc.scalar.activation(
-                        out=squares[:],
-                        in_=act[gate][:, t, :],
-                        func=ACT.Square,
-                        bias=live["sums", g][:, col : col + 1],
-                        scale=-1.0 * FEAT,
-                        accum_out=sq_dev[:, col : col + 1],
-                    )
-            neg_mean = stats.tile([P, TILES * GATES], F32, name="neg_mean")
-            nc.scalar.mul(out=neg_mean[:], in_=live["sums", g][:], mul=-1.0 / FEAT)
-            live["neg_mean", g] = neg_mean
-            live["sq_dev", g] = sq_dev
+        def deviations(g, t):
+            if t == 0:
+                live["sq_dev", g] = stats.tile([P, TILES * GATES], F32, name="sq_dev")
+            for gate in range(GATES):
+                col = GATES * t + gate
+                squares = acts.tile([P, FEAT], F32, name="squares")
+                nc.scalar.activation(
+                    out=squares[:],
+                    in_=live["act", g][:, gate, t, :],
+                    func=ACT.Square,
+                    bias=live["sums", g][:, col : col + 1],
+                    scale=-1.0 * FEAT,
+                    accum_out=live["sq_dev", g][:, col : col + 1],
+                )
+            if t == TILES - 1:
+                neg_mean = stats.tile([P, TILES * GATES], F32, name="neg_mean")
+                nc.scalar.mul(out=neg_mean[:], in_=live["sums", g][:], mul=-1.0 / FEAT)
+                live["neg_mean", g] = neg_mean
 
-        def centre_and_gain(g):
-            for t in range(TILES):
-                for gate in range(GATES):
-                    col = GATES * t + gate
-                    nc.vector.scalar_tensor_tensor(
-                        out=live["act", g][gate][:, t, :],
-                        in0=live["act", g][gate][:, t, :],
-                        scalar=live["neg_mean", g][:, col : col + 1],
-                        in1=gain_shift[gate][:, 0:FEAT],
-                        op0=ALU.add,
-                        op1=ALU.mult,
-                    )
-
-        def inverse_std(g):
+        def normalise(g):
             var_eps = stats.tile([P, TILES * GATES], F32, name="var_eps")
             rstd = stats.tile([P, TILES * GATES], F32, name="rstd")
             nc.gpsimd.tensor_scalar(
                 out=var_eps[:], in0=live["sq_dev", g][:], scalar1=1.0 / FEAT**3, scalar2=EPS, op0=ALU.mult, op1=ALU.add
             )
             nc.gpsimd.tensor_tensor(out=rstd[:], in0=var_eps[:], in1=neg_half[:], op=ALU.pow)
-            live["rstd", g] = rstd
-
-        def scale_and_shift(g):
             for gate in range(GATES):
                 for t in range(TILES):
                     col = GATES * t + gate
-                    nc.vector.scalar_tensor_tensor(
-                        out=live["act", g][gate][:, t, :],
-                        in0=live["act", g][gate][:, t, :],
-                        scalar=live["rstd", g][:, col : col + 1],
-                        in1=gain_shift[gate][:, FEAT : 2 * FEAT],
-                        op0=ALU.mult,
-                        op1=ALU.add,
+                    act = live["act", g][:, gate, t, :]
+                    nc.gpsimd.tensor_scalar(
+                        out=act,
+                        in0=act,
+                        scalar1=live["neg_mean", g][:, col : col + 1],
+                        scalar2=rstd[:, col : col + 1],
+                        op0=ALU.add,
+                        op1=ALU.mult,
                     )
 
-        def sigmoids(g):
-            for gate in range(GATES):
-                nc.scalar.activation(out=live["act", g][gate][:], in_=live["act", g][gate][:], func=ACT.Sigmoid)
+        def gate_sigmoid(g, gate):
+            sig = acts.tile([P, BLOCKS, TILES, P], F32, name="sig%d" % gate)
+            for half in range(BLOCKS // 2):
+                norm = psum.tile([P, 2, TILES, P], F32, name="norm", tag="norm")
+                for b in range(2):
+                    block = 2 * half + b
+                    for t in range(TILES):
+                        nc.tensor.transpose(
+                            out=norm[:, b, t, :],
+                            in_=live["act", g][:, gate, t, block * P : (block + 1) * P],
+                            identity=ident[:],
+                        )
+                for b in range(2):
+                    block = 2 * half + b
+                    gain = 2 * gate * BLOCKS + block
+                    shift = gain + BLOCKS
+                    nc.scalar.activation(
+                        out=sig[:, block],
+                        in_=norm[:, b],
+                        func=ACT.Sigmoid,
+                        scale=affine[:, gain : gain + 1],
+                        bias=affine[:, shift : shift + 1],
+                    )
+            live["sig", g, gate] = sig
 
-        def updater(g):
-            return nc.vector if (GROUPS - 1 - g) % VECTOR_EVERY == 0 else nc.gpsimd
+        def gate_back(g, gate, t):
+            bank = psum.tile([P, BLOCKS, P], F32, name="back", tag="back")
+            for block in range(BLOCKS):
+                nc.tensor.transpose(
+                    out=bank[:, block, :], in_=live["sig", g, gate][:, block, t, :], identity=ident[:]
+                )
+            return bank[:].rearrange("p b f -> p (b f)")
 
         def new_cell(g):
-            cell = live["act", g][0][:].rearrange("p t f -> p (t f)")
-            updater(g).tensor_tensor(out=cell, in0=cell, in1=live["c_old", g][:], op=ALU.mult)
-            updater(g).tensor_tensor(out=cell, in0=cell, in1=live["ic", g][:], op=ALU.add)
-            tanh_c = acts.tile([P, TILES * FEAT], F32, name="tanh_c")
-            nc.scalar.activation(out=tanh_c[:], in_=cell, func=ACT.Tanh)
-            nc.sync.dma_start(out=c_new_rows[g], in_=cell)
+            cell = acts.tile([P, TILES, FEAT], F32, name="cell")
+            for t in range(TILES):
+                nc.vector.tensor_tensor(
+                    out=cell[:, t, :], in0=gate_back(g, 0, t), in1=live["c_old", g][:, t, :], op=ALU.mult
+                )
+            for t in range(TILES):
+                nc.gpsimd.tensor_tensor(
+                    out=cell[:, t, :], in0=cell[:, t, :], in1=live["ic", g][:, t, :], op=ALU.add
+                )
+            nc.sync.dma_start(out=c_new_rows[g], in_=cell[:].rearrange("p t f -> p (t f)"))
+            live["cell", g] = cell
+
+        def cell_tanh(g):
+            tanh_c = acts.tile([P, TILES, FEAT], F32, name="tanh_c")
+            nc.scalar.activation(out=tanh_c[:], in_=live["cell", g][:], func=ACT.Tanh)
             live["tanh_c", g] = tanh_c
 
         def new_hidden(g):
-            hidden = live["act", g][1][:].rearrange("p t f -> p (t f)")
-            updater(g).tensor_tensor(out=hidden, in0=hidden, in1=live["tanh_c", g][:], op=ALU.mult)
-            nc.sync.dma_start(out=h_new_rows[g], in_=hidden)
+            hidden = acts.tile([P, TILES, FEAT], F32, name="hidden")
+            for t in range(TILES):
+                nc.vector.tensor_tensor(
+                    out=hidden[:, t, :], in0=gate_back(g, 1, t), in1=live["tanh_c", g][:, t, :], op=ALU.mult
+                )
+            nc.sync.dma_start(out=h_new_rows[g], in_=hidden[:].rearrange("p t f -> p (t f)"))
 
-        def at(stage, g):
+        def at(stage, g, *args):
             if 0 <= g < GROUPS:
-                stage(g)
+                stage(g, *args)
 
-        for step in range(-3, GROUPS + 3):
-            at(load_operands, step + 3)
-            at(load_cell, step)
-            at(regroup_operands, step + 1)
-            at(transpose_operands, step + 2)
-            at(add_bias, step)
-            at(deviations, step)
+        for step in range(-4, GROUPS + 4):
+            at(load_operands, step + 4)
+            at(load_cell, step - 1)
+            at(cell_tanh, step - 4)
+            at(multiply, step, 0)
+            at(deviations, step, 0)
+            at(new_hidden, step - 4)
+            at(gate_sigmoid, step - 2, 0)
+            at(transpose_operands, step + 2, 0)
+            at(normalise, step - 1)
+            at(multiply, step, 1)
+            at(deviations, step, 1)
+            at(new_cell, step - 3)
+            at(gate_sigmoid, step - 2, 1)
+            at(transpose_operands, step + 2, 1)
             at(quantise_operands, step + 1)
-            at(multiply, step + 1)
-            at(scale_and_shift, step - 1)
-            at(sigmoids, step - 1)
-            at(centre_and_gain, step)
-            at(new_cell, step - 2)
-            at(inverse_std, step)
-            at(new_hidden, step - 3)

@@ -129,17 +129,20 @@ def tile_layernormlstmcell_pb_t_kernel(
             live["c_old", g] = c_old
             live["ic", g] = ic
 
-        def transpose_operands(g, t):
+        def transpose_operand(g, t, operand):
             words = live["xh", g][:].bitcast(F32)
-            turned = psum.tile([P, 4, P], F32, name="turned", tag="turned")
-            for operand in range(2):
-                for u in range(2):
-                    first = (operand * TILES + t) * WORDS
-                    nc.tensor.transpose(
-                        out=turned[:, 2 * operand + u, :],
-                        in_=words[:, first + u : first + WORDS : 2],
-                        identity=ident[:],
-                    )
+            if operand == 0:
+                live["turned", g, t] = psum.tile([P, 4, P], F32, name="turned", tag="turned")
+            turned = live["turned", g, t]
+            for u in range(2):
+                first = (operand * TILES + t) * WORDS
+                nc.tensor.transpose(
+                    out=turned[:, 2 * operand + u, :],
+                    in_=words[:, first + u : first + WORDS : 2],
+                    identity=ident[:],
+                )
+            if operand == 0:
+                return
             if t == 0:
                 live["grouped", g] = mxin.tile([P, TILES * 2 * P * 4], BF16, name="grouped", align_bytes=64)
             grouped_words = live["grouped", g][:].bitcast(F32).rearrange(
@@ -155,51 +158,49 @@ def tile_layernormlstmcell_pb_t_kernel(
             live["codes", g] = codes
             live["scales", g] = scales
 
-        def multiply(g, t):
+        def multiply(g, t, gate):
             codes, scales = live["codes", g], live["scales", g]
-            if t == 0:
+            if t == 0 and gate == 0:
                 live["act", g] = acts.tile([P, GATES, TILES, FEAT], F32, name="act")
                 live["sums", g] = stats.tile([P, TILES * GATES], F32, name="sums")
-            for gate in range(GATES):
-                acc = psum.tile([P, FEAT], F32, name="acc", tag="acc")
-                for operand in range(2):
-                    r_cols = slice((2 * t + operand) * P, (2 * t + operand + 1) * P)
-                    w_cols = slice((2 * gate + operand) * FEAT, (2 * gate + operand + 1) * FEAT)
-                    nc.tensor.matmul_mx(
-                        out=acc[:],
-                        lhsT=codes[:, r_cols].bitcast(FP8X4),
-                        lhsT_scale=scales[:, r_cols],
-                        rhs=w_codes[:, w_cols].bitcast(FP8X4),
-                        rhs_scale=w_scales[:, w_cols],
-                        start=(operand == 0),
-                        stop=(operand == 1),
-                    )
-                col = GATES * t + gate
-                nc.vector.scalar_tensor_tensor(
-                    out=live["act", g][:, gate, t, :],
-                    in0=acc[:],
-                    scalar=1.0,
-                    in1=bias[:, gate * FEAT : (gate + 1) * FEAT],
-                    op0=ALU.mult,
-                    op1=ALU.add,
-                    accum_out=live["sums", g][:, col : col + 1],
+            acc = psum.tile([P, FEAT], F32, name="acc", tag="acc")
+            for operand in range(2):
+                r_cols = slice((2 * t + operand) * P, (2 * t + operand + 1) * P)
+                w_cols = slice((2 * gate + operand) * FEAT, (2 * gate + operand + 1) * FEAT)
+                nc.tensor.matmul_mx(
+                    out=acc[:],
+                    lhsT=codes[:, r_cols].bitcast(FP8X4),
+                    lhsT_scale=scales[:, r_cols],
+                    rhs=w_codes[:, w_cols].bitcast(FP8X4),
+                    rhs_scale=w_scales[:, w_cols],
+                    start=(operand == 0),
+                    stop=(operand == 1),
                 )
+            col = GATES * t + gate
+            nc.vector.scalar_tensor_tensor(
+                out=live["act", g][:, gate, t, :],
+                in0=acc[:],
+                scalar=1.0,
+                in1=bias[:, gate * FEAT : (gate + 1) * FEAT],
+                op0=ALU.mult,
+                op1=ALU.add,
+                accum_out=live["sums", g][:, col : col + 1],
+            )
 
-        def deviations(g, t):
-            if t == 0:
+        def deviations(g, t, gate):
+            if t == 0 and gate == 0:
                 live["sq_dev", g] = stats.tile([P, TILES * GATES], F32, name="sq_dev")
-            for gate in range(GATES):
-                col = GATES * t + gate
-                squares = acts.tile([P, FEAT], F32, name="squares")
-                nc.scalar.activation(
-                    out=squares[:],
-                    in_=live["act", g][:, gate, t, :],
-                    func=ACT.Square,
-                    bias=live["sums", g][:, col : col + 1],
-                    scale=-1.0 * FEAT,
-                    accum_out=live["sq_dev", g][:, col : col + 1],
-                )
-            if t == TILES - 1:
+            col = GATES * t + gate
+            squares = acts.tile([P, FEAT], F32, name="squares")
+            nc.scalar.activation(
+                out=squares[:],
+                in_=live["act", g][:, gate, t, :],
+                func=ACT.Square,
+                bias=live["sums", g][:, col : col + 1],
+                scale=-1.0 * FEAT,
+                accum_out=live["sq_dev", g][:, col : col + 1],
+            )
+            if t == TILES - 1 and gate == GATES - 1:
                 neg_mean = stats.tile([P, TILES * GATES], F32, name="neg_mean")
                 nc.scalar.mul(out=neg_mean[:], in_=live["sums", g][:], mul=-1.0 / FEAT)
                 live["neg_mean", g] = neg_mean
@@ -224,30 +225,29 @@ def tile_layernormlstmcell_pb_t_kernel(
                         op1=ALU.mult,
                     )
 
-        def gate_sigmoid(g, gate):
-            sig = acts.tile([P, BLOCKS, TILES, P], F32, name="sig%d" % gate)
-            for half in range(BLOCKS // 2):
-                norm = psum.tile([P, 2, TILES, P], F32, name="norm", tag="norm")
-                for b in range(2):
-                    block = 2 * half + b
-                    for t in range(TILES):
-                        nc.tensor.transpose(
-                            out=norm[:, b, t, :],
-                            in_=live["act", g][:, gate, t, block * P : (block + 1) * P],
-                            identity=ident[:],
-                        )
-                for b in range(2):
-                    block = 2 * half + b
-                    gain = 2 * gate * BLOCKS + block
-                    shift = gain + BLOCKS
-                    nc.scalar.activation(
-                        out=sig[:, block],
-                        in_=norm[:, b],
-                        func=ACT.Sigmoid,
-                        scale=affine[:, gain : gain + 1],
-                        bias=affine[:, shift : shift + 1],
+        def gate_sigmoid(g, gate, half):
+            if half == 0:
+                live["sig", g, gate] = acts.tile([P, BLOCKS, TILES, P], F32, name="sig%d" % gate)
+            norm = psum.tile([P, 2, TILES, P], F32, name="norm", tag="norm")
+            for b in range(2):
+                block = 2 * half + b
+                for t in range(TILES):
+                    nc.tensor.transpose(
+                        out=norm[:, b, t, :],
+                        in_=live["act", g][:, gate, t, block * P : (block + 1) * P],
+                        identity=ident[:],
                     )
-            live["sig", g, gate] = sig
+            for b in range(2):
+                block = 2 * half + b
+                gain = 2 * gate * BLOCKS + block
+                shift = gain + BLOCKS
+                nc.scalar.activation(
+                    out=live["sig", g, gate][:, block],
+                    in_=norm[:, b],
+                    func=ACT.Sigmoid,
+                    scale=affine[:, gain : gain + 1],
+                    bias=affine[:, shift : shift + 1],
+                )
 
         def gate_back(g, gate, t):
             bank = psum.tile([P, BLOCKS, P], F32, name="back", tag="back")
@@ -257,31 +257,31 @@ def tile_layernormlstmcell_pb_t_kernel(
                 )
             return bank[:].rearrange("p b f -> p (b f)")
 
-        def new_cell(g):
-            cell = acts.tile([P, TILES, FEAT], F32, name="cell")
-            for t in range(TILES):
-                nc.vector.tensor_tensor(
-                    out=cell[:, t, :], in0=gate_back(g, 0, t), in1=live["c_old", g][:, t, :], op=ALU.mult
-                )
-            for t in range(TILES):
-                nc.gpsimd.tensor_tensor(
-                    out=cell[:, t, :], in0=cell[:, t, :], in1=live["ic", g][:, t, :], op=ALU.add
-                )
-            nc.sync.dma_start(out=c_new_rows[g], in_=cell[:].rearrange("p t f -> p (t f)"))
-            live["cell", g] = cell
+        def new_cell(g, t):
+            if t == 0:
+                live["cell", g] = acts.tile([P, TILES, FEAT], F32, name="cell")
+            cell = live["cell", g]
+            nc.vector.tensor_tensor(
+                out=cell[:, t, :], in0=gate_back(g, 0, t), in1=live["c_old", g][:, t, :], op=ALU.mult
+            )
+            nc.gpsimd.tensor_tensor(out=cell[:, t, :], in0=cell[:, t, :], in1=live["ic", g][:, t, :], op=ALU.add)
+            if t == TILES - 1:
+                nc.sync.dma_start(out=c_new_rows[g], in_=cell[:].rearrange("p t f -> p (t f)"))
 
         def cell_tanh(g):
             tanh_c = acts.tile([P, TILES, FEAT], F32, name="tanh_c")
             nc.scalar.activation(out=tanh_c[:], in_=live["cell", g][:], func=ACT.Tanh)
             live["tanh_c", g] = tanh_c
 
-        def new_hidden(g):
-            hidden = acts.tile([P, TILES, FEAT], F32, name="hidden")
-            for t in range(TILES):
-                nc.vector.tensor_tensor(
-                    out=hidden[:, t, :], in0=gate_back(g, 1, t), in1=live["tanh_c", g][:, t, :], op=ALU.mult
-                )
-            nc.sync.dma_start(out=h_new_rows[g], in_=hidden[:].rearrange("p t f -> p (t f)"))
+        def new_hidden(g, t):
+            if t == 0:
+                live["hidden", g] = acts.tile([P, TILES, FEAT], F32, name="hidden")
+            hidden = live["hidden", g]
+            nc.vector.tensor_tensor(
+                out=hidden[:, t, :], in0=gate_back(g, 1, t), in1=live["tanh_c", g][:, t, :], op=ALU.mult
+            )
+            if t == TILES - 1:
+                nc.sync.dma_start(out=h_new_rows[g], in_=hidden[:].rearrange("p t f -> p (t f)"))
 
         def at(stage, g, *args):
             if 0 <= g < GROUPS:
@@ -291,15 +291,16 @@ def tile_layernormlstmcell_pb_t_kernel(
             at(load_operands, step + 4)
             at(load_cell, step - 1)
             at(cell_tanh, step - 4)
-            at(multiply, step, 0)
-            at(deviations, step, 0)
-            at(new_hidden, step - 4)
-            at(gate_sigmoid, step - 2, 0)
-            at(transpose_operands, step + 2, 0)
-            at(normalise, step - 1)
-            at(multiply, step, 1)
-            at(deviations, step, 1)
-            at(new_cell, step - 3)
-            at(gate_sigmoid, step - 2, 1)
-            at(transpose_operands, step + 2, 1)
+            for quarter in range(4):
+                hi, lo = quarter // 2, quarter % 2
+                at(multiply, step, hi, lo)
+                at(deviations, step, hi, lo)
+                if hi == 0:
+                    at(new_hidden, step - 4, lo)
+                else:
+                    at(new_cell, step - 3, lo)
+                at(gate_sigmoid, step - 2, hi, lo)
+                at(transpose_operand, step + 2, hi, lo)
+                if quarter == 0:
+                    at(normalise, step - 1)
             at(quantise_operands, step + 1)

@@ -35,8 +35,9 @@ def tile_layernormlstmcell_pb_t_kernel(
         wstage = ctx.enter_context(tc.tile_pool(name="wstage", bufs=2))
         loads = ctx.enter_context(tc.tile_pool(name="loads", bufs=4))
         mxin = ctx.enter_context(tc.tile_pool(name="mxin", bufs=3))
-        stats = ctx.enter_context(tc.tile_pool(name="stats", bufs=4))
-        acts = ctx.enter_context(tc.tile_pool(name="acts", bufs=4))
+        stats = ctx.enter_context(tc.tile_pool(name="stats", bufs=5))
+        acts = ctx.enter_context(tc.tile_pool(name="acts", bufs=5))
+        scrap = ctx.enter_context(tc.tile_pool(name="scrap", bufs=2))
         psum = ctx.enter_context(tc.psum_pool(name="psum", bufs=2))
 
         ident = consts.tile([P, P], F32)
@@ -191,7 +192,7 @@ def tile_layernormlstmcell_pb_t_kernel(
             if t == 0 and gate == 0:
                 live["sq_dev", g] = stats.tile([P, TILES * GATES], F32, name="sq_dev")
             col = GATES * t + gate
-            squares = acts.tile([P, FEAT], F32, name="squares")
+            squares = scrap.tile([P, FEAT], F32, name="squares")
             nc.scalar.activation(
                 out=squares[:],
                 in_=live["act", g][:, gate, t, :],
@@ -205,25 +206,27 @@ def tile_layernormlstmcell_pb_t_kernel(
                 nc.scalar.mul(out=neg_mean[:], in_=live["sums", g][:], mul=-1.0 / FEAT)
                 live["neg_mean", g] = neg_mean
 
-        def normalise(g):
+        def inverse_std(g):
             var_eps = stats.tile([P, TILES * GATES], F32, name="var_eps")
             rstd = stats.tile([P, TILES * GATES], F32, name="rstd")
             nc.gpsimd.tensor_scalar(
                 out=var_eps[:], in0=live["sq_dev", g][:], scalar1=1.0 / FEAT**3, scalar2=EPS, op0=ALU.mult, op1=ALU.add
             )
             nc.gpsimd.tensor_tensor(out=rstd[:], in0=var_eps[:], in1=neg_half[:], op=ALU.pow)
-            for gate in range(GATES):
-                for t in range(TILES):
-                    col = GATES * t + gate
-                    act = live["act", g][:, gate, t, :]
-                    nc.gpsimd.tensor_scalar(
-                        out=act,
-                        in0=act,
-                        scalar1=live["neg_mean", g][:, col : col + 1],
-                        scalar2=rstd[:, col : col + 1],
-                        op0=ALU.add,
-                        op1=ALU.mult,
-                    )
+            live["rstd", g] = rstd
+
+        def normalise(g, gate):
+            for t in range(TILES):
+                col = GATES * t + gate
+                act = live["act", g][:, gate, t, :]
+                nc.gpsimd.tensor_scalar(
+                    out=act,
+                    in0=act,
+                    scalar1=live["neg_mean", g][:, col : col + 1],
+                    scalar2=live["rstd", g][:, col : col + 1],
+                    op0=ALU.add,
+                    op1=ALU.mult,
+                )
 
         def gate_sigmoid(g, gate, half):
             if half == 0:
@@ -257,16 +260,19 @@ def tile_layernormlstmcell_pb_t_kernel(
                 )
             return bank[:].rearrange("p b f -> p (b f)")
 
-        def new_cell(g, t):
+        def keep_cell(g, t):
             if t == 0:
                 live["cell", g] = acts.tile([P, TILES, FEAT], F32, name="cell")
             cell = live["cell", g]
             nc.vector.tensor_tensor(
                 out=cell[:, t, :], in0=gate_back(g, 0, t), in1=live["c_old", g][:, t, :], op=ALU.mult
             )
-            nc.gpsimd.tensor_tensor(out=cell[:, t, :], in0=cell[:, t, :], in1=live["ic", g][:, t, :], op=ALU.add)
-            if t == TILES - 1:
-                nc.sync.dma_start(out=c_new_rows[g], in_=cell[:].rearrange("p t f -> p (t f)"))
+
+        def add_candidate(g):
+            cell = live["cell", g]
+            for t in range(TILES):
+                nc.gpsimd.tensor_tensor(out=cell[:, t, :], in0=cell[:, t, :], in1=live["ic", g][:, t, :], op=ALU.add)
+            nc.sync.dma_start(out=c_new_rows[g], in_=cell[:].rearrange("p t f -> p (t f)"))
 
         def cell_tanh(g):
             tanh_c = acts.tile([P, TILES, FEAT], F32, name="tanh_c")
@@ -287,20 +293,32 @@ def tile_layernormlstmcell_pb_t_kernel(
             if 0 <= g < GROUPS:
                 stage(g, *args)
 
-        for step in range(-4, GROUPS + 4):
+        for step in range(-4, GROUPS + 5):
             at(load_operands, step + 4)
             at(load_cell, step - 1)
-            at(cell_tanh, step - 4)
-            for quarter in range(4):
-                hi, lo = quarter // 2, quarter % 2
-                at(multiply, step, hi, lo)
-                at(deviations, step, hi, lo)
-                if hi == 0:
-                    at(new_hidden, step - 4, lo)
-                else:
-                    at(new_cell, step - 3, lo)
-                at(gate_sigmoid, step - 2, hi, lo)
-                at(transpose_operand, step + 2, hi, lo)
-                if quarter == 0:
-                    at(normalise, step - 1)
+            at(multiply, step, 0, 0)
+            at(multiply, step, 0, 1)
+            at(deviations, step - 1, 1, 0)
+            at(deviations, step - 1, 1, 1)
+            at(keep_cell, step - 3, 0)
+            at(keep_cell, step - 3, 1)
+            at(gate_sigmoid, step - 3, 1, 0)
+            at(gate_sigmoid, step - 3, 1, 1)
             at(quantise_operands, step + 1)
+            at(transpose_operand, step + 2, 0, 0)
+            at(transpose_operand, step + 2, 0, 1)
+            at(normalise, step - 2, 1)
+            at(cell_tanh, step - 4)
+            at(multiply, step, 1, 0)
+            at(multiply, step, 1, 1)
+            at(deviations, step, 0, 0)
+            at(deviations, step, 0, 1)
+            at(new_hidden, step - 4, 0)
+            at(new_hidden, step - 4, 1)
+            at(gate_sigmoid, step - 2, 0, 0)
+            at(gate_sigmoid, step - 2, 0, 1)
+            at(transpose_operand, step + 2, 1, 0)
+            at(transpose_operand, step + 2, 1, 1)
+            at(inverse_std, step - 1)
+            at(normalise, step - 1, 0)
+            at(add_candidate, step - 3)

@@ -297,27 +297,27 @@ def tile_layernormlstmcell_pb_t_kernel(
             at(load_operands, step + 4)
             at(load_cell, step - 1)
             at(multiply, step, 0, 0)
-            at(multiply, step, 0, 1)
-            at(deviations, step - 1, 1, 0)
-            at(deviations, step - 1, 1, 1)
-            at(keep_cell, step - 3, 0)
-            at(keep_cell, step - 3, 1)
             at(gate_sigmoid, step - 3, 1, 0)
-            at(gate_sigmoid, step - 3, 1, 1)
-            at(quantise_operands, step + 1)
+            at(keep_cell, step - 3, 0)
+            at(deviations, step - 1, 1, 0)
             at(transpose_operand, step + 2, 0, 0)
+            at(multiply, step, 0, 1)
+            at(gate_sigmoid, step - 3, 1, 1)
+            at(keep_cell, step - 3, 1)
+            at(deviations, step - 1, 1, 1)
+            at(quantise_operands, step + 1)
             at(transpose_operand, step + 2, 0, 1)
             at(normalise, step - 2, 1)
             at(cell_tanh, step - 4)
             at(multiply, step, 1, 0)
-            at(multiply, step, 1, 1)
-            at(deviations, step, 0, 0)
-            at(deviations, step, 0, 1)
-            at(new_hidden, step - 4, 0)
-            at(new_hidden, step - 4, 1)
             at(gate_sigmoid, step - 2, 0, 0)
-            at(gate_sigmoid, step - 2, 0, 1)
+            at(deviations, step, 0, 0)
+            at(new_hidden, step - 4, 0)
             at(transpose_operand, step + 2, 1, 0)
+            at(multiply, step, 1, 1)
+            at(gate_sigmoid, step - 2, 0, 1)
+            at(deviations, step, 0, 1)
+            at(new_hidden, step - 4, 1)
             at(transpose_operand, step + 2, 1, 1)
             at(inverse_std, step - 1)
             at(normalise, step - 1, 0)

@@ -58,25 +58,31 @@ def tile_layernormlstmcell_pb_t_kernel(
         w_codes = consts.tile([P, 4 * FEAT], U32, align_bytes=64)
         w_scales = consts.tile([P, 4 * FEAT], U8, align_bytes=64)
         raws = []
-        for w, weight in enumerate((Wf_w, Uf_w, Wo_w, Uo_w)):
-            raw = consts.tile([P, 4 * K], BF16, name="raw%d" % w)
+
+        def load_weight(weight):
+            raw = consts.tile([P, 4 * K], BF16, name="raw%d" % len(raws))
             nc.sync.dma_start(
                 out=raw[:].rearrange("p (b k) -> p b k", b=4),
                 in_=weight.rearrange("(b p) k -> p b k", p=P),
             )
             raws.append(raw)
-        for v, vec in enumerate((Wf_b, Wo_b)):
-            nc.sync.dma_start(out=bias_rows[0:1, v * FEAT : (v + 1) * FEAT], in_=vec.unsqueeze(0))
-        for v, vec in enumerate((lnf_g, lnf_b, lno_g, lno_b)):
-            nc.sync.dma_start(
-                out=affine_rows[BLOCKS * v : BLOCKS * (v + 1), :], in_=vec.rearrange("(j p) -> j p", p=P)
-            )
-        for w in range(4):
+
+        def load_biases():
+            for v, vec in enumerate((Wf_b, Wo_b)):
+                nc.sync.dma_start(out=bias_rows[0:1, v * FEAT : (v + 1) * FEAT], in_=vec.unsqueeze(0))
+
+        def load_affine():
+            for v, vec in enumerate((lnf_g, lnf_b, lno_g, lno_b)):
+                nc.sync.dma_start(
+                    out=affine_rows[BLOCKS * v : BLOCKS * (v + 1), :], in_=vec.rearrange("(j p) -> j p", p=P)
+                )
+
+        def prepare_weight(w):
             raw_words = raws[w][:].bitcast(F32)
-            grouped = wstage.tile([P, 4 * FEAT], BF16, align_bytes=64)
+            grouped = wstage.tile([P, 4 * FEAT], BF16, name="w_grouped", align_bytes=64)
             grouped_words = grouped[:].bitcast(F32).rearrange("p (j u) -> p j u", u=2)
             for half in range(2):
-                turned = psum.tile([P, 2, 2 * P], F32, tag="turned")
+                turned = psum.tile([P, 2, 2 * P], F32, name="w_turned", tag=("turned", "norm", "back", "acc")[w])
                 for u in range(2):
                     for b in range(2):
                         first = (2 * half + b) * WORDS
@@ -96,16 +102,21 @@ def tile_layernormlstmcell_pb_t_kernel(
                 in_=grouped[:],
             )
 
-        bias_ps = psum.tile([P, GATES * FEAT], BF16, name="bias_ps", tag="acc")
         bias = consts.tile([P, GATES * FEAT], BF16)
-        for gate in range(GATES):
-            cols = slice(gate * FEAT, (gate + 1) * FEAT)
-            nc.tensor.matmul(out=bias_ps[:, cols], lhsT=ones[:], rhs=bias_rows[:, cols], start=True, stop=True)
-        nc.vector.tensor_copy(out=bias[:], in_=bias_ps[:])
-        affine_ps = psum.tile([P, GATES * FEAT], BF16, name="affine_ps", tag="back")
-        nc.tensor.transpose(out=affine_ps[:, 0:P], in_=affine_rows[:], identity=ident_bf16[:])
+
+        def spread_biases():
+            bias_ps = psum.tile([P, GATES * FEAT], BF16, name="bias_ps", tag="acc")
+            for gate in range(GATES):
+                cols = slice(gate * FEAT, (gate + 1) * FEAT)
+                nc.tensor.matmul(out=bias_ps[:, cols], lhsT=ones[:], rhs=bias_rows[:, cols], start=True, stop=True)
+            nc.scalar.copy(out=bias[:], in_=bias_ps[:])
+
         affine = consts.tile([P, 4 * BLOCKS], F32)
-        nc.vector.tensor_copy(out=affine[:], in_=affine_ps[:, 0 : 4 * BLOCKS])
+
+        def turn_affine():
+            affine_ps = psum.tile([P, GATES * FEAT], BF16, name="affine_ps", tag="back")
+            nc.tensor.transpose(out=affine_ps[:, 0:P], in_=affine_rows[:], identity=ident_bf16[:])
+            nc.vector.tensor_copy(out=affine[:], in_=affine_ps[:, 0 : 4 * BLOCKS])
 
         rows = "(g p t) k -> g p (t k)"
         x_rows = x.rearrange(rows, p=P, t=TILES)
@@ -219,7 +230,7 @@ def tile_layernormlstmcell_pb_t_kernel(
             for t in range(TILES):
                 col = GATES * t + gate
                 act = live["act", g][:, gate, t, :]
-                nc.gpsimd.tensor_scalar(
+                (nc.vector if gate or g >= GROUPS - 1 else nc.gpsimd).tensor_scalar(
                     out=act,
                     in0=act,
                     scalar1=live["neg_mean", g][:, col : col + 1],
@@ -271,7 +282,7 @@ def tile_layernormlstmcell_pb_t_kernel(
         def add_candidate(g):
             cell = live["cell", g]
             for t in range(TILES):
-                nc.gpsimd.tensor_tensor(out=cell[:, t, :], in0=cell[:, t, :], in1=live["ic", g][:, t, :], op=ALU.add)
+                (nc.vector if g >= GROUPS - 1 else nc.gpsimd).tensor_tensor(out=cell[:, t, :], in0=cell[:, t, :], in1=live["ic", g][:, t, :], op=ALU.add)
             nc.sync.dma_start(out=c_new_rows[g], in_=cell[:].rearrange("p t f -> p (t f)"))
 
         def cell_tanh(g):
@@ -293,7 +304,7 @@ def tile_layernormlstmcell_pb_t_kernel(
             if 0 <= g < GROUPS:
                 stage(g, *args)
 
-        for step in range(-4, GROUPS + 5):
+        def run_step(step):
             at(load_operands, step + 4)
             at(load_cell, step - 1)
             at(multiply, step, 0, 0)
@@ -305,7 +316,8 @@ def tile_layernormlstmcell_pb_t_kernel(
             at(gate_sigmoid, step - 3, 1, 1)
             at(keep_cell, step - 3, 1)
             at(deviations, step - 1, 1, 1)
-            at(quantise_operands, step + 1)
+            if step >= 0:
+                at(quantise_operands, step + 1)
             at(transpose_operand, step + 2, 0, 1)
             at(normalise, step - 2, 1)
             at(cell_tanh, step - 4)
@@ -322,3 +334,26 @@ def tile_layernormlstmcell_pb_t_kernel(
             at(inverse_std, step - 1)
             at(normalise, step - 1, 0)
             at(add_candidate, step - 3)
+
+        load_weight(Wf_w)
+        load_biases()
+        load_weight(Uf_w)
+        load_operands(0)
+        load_weight(Wo_w)
+        load_weight(Uo_w)
+        load_affine()
+        load_operands(1)
+        load_operands(2)
+        prepare_weight(0)
+        prepare_weight(1)
+        transpose_operand(0, 0, 0)
+        transpose_operand(0, 0, 1)
+        transpose_operand(0, 1, 0)
+        transpose_operand(0, 1, 1)
+        prepare_weight(2)
+        quantise_operands(0)
+        spread_biases()
+        prepare_weight(3)
+        turn_affine()
+        for step in range(-1, GROUPS + 5):
+            run_step(step)

@@ -105,7 +105,7 @@ def tile_layernormlstmcell_pb_t_kernel(
         bias = consts.tile([P, GATES * FEAT], BF16)
 
         def spread_biases():
-            bias_ps = psum.tile([P, GATES * FEAT], BF16, name="bias_ps", tag="acc")
+            bias_ps = psum.tile([P, GATES * FEAT], BF16, name="bias_ps", tag="norm")
             for gate in range(GATES):
                 cols = slice(gate * FEAT, (gate + 1) * FEAT)
                 nc.tensor.matmul(out=bias_ps[:, cols], lhsT=ones[:], rhs=bias_rows[:, cols], start=True, stop=True)
@@ -212,12 +212,13 @@ def tile_layernormlstmcell_pb_t_kernel(
                 scale=-1.0 * FEAT,
                 accum_out=live["sq_dev", g][:, col : col + 1],
             )
-            if t == TILES - 1 and gate == GATES - 1:
-                neg_mean = stats.tile([P, TILES * GATES], F32, name="neg_mean")
-                nc.scalar.mul(out=neg_mean[:], in_=live["sums", g][:], mul=-1.0 / FEAT)
-                live["neg_mean", g] = neg_mean
 
-        def inverse_std(g):
+        def mean_and_inverse_std(g):
+            neg_mean = stats.tile([P, TILES * GATES], F32, name="neg_mean")
+            nc.gpsimd.tensor_scalar(
+                out=neg_mean[:], in0=live["sums", g][:], scalar1=-1.0 / FEAT, scalar2=0.0, op0=ALU.mult, op1=ALU.add
+            )
+            live["neg_mean", g] = neg_mean
             var_eps = stats.tile([P, TILES * GATES], F32, name="var_eps")
             rstd = stats.tile([P, TILES * GATES], F32, name="rstd")
             nc.gpsimd.tensor_scalar(
@@ -230,7 +231,7 @@ def tile_layernormlstmcell_pb_t_kernel(
             for t in range(TILES):
                 col = GATES * t + gate
                 act = live["act", g][:, gate, t, :]
-                (nc.vector if gate or g >= GROUPS - 1 else nc.gpsimd).tensor_scalar(
+                (nc.vector if gate == 0 or g >= GROUPS - 1 else nc.gpsimd).tensor_scalar(
                     out=act,
                     in0=act,
                     scalar1=live["neg_mean", g][:, col : col + 1],
@@ -308,32 +309,32 @@ def tile_layernormlstmcell_pb_t_kernel(
             at(load_operands, step + 4)
             at(load_cell, step - 1)
             at(multiply, step, 0, 0)
-            at(gate_sigmoid, step - 3, 1, 0)
-            at(keep_cell, step - 3, 0)
-            at(deviations, step - 1, 1, 0)
-            at(transpose_operand, step + 2, 0, 0)
-            at(multiply, step, 0, 1)
-            at(gate_sigmoid, step - 3, 1, 1)
-            at(keep_cell, step - 3, 1)
+            at(gate_sigmoid, step - 2, 0, 0)
             at(deviations, step - 1, 1, 1)
+            at(new_hidden, step - 4, 0)
+            at(transpose_operand, step + 2, 0, 0)
             if step >= 0:
                 at(quantise_operands, step + 1)
-            at(transpose_operand, step + 2, 0, 1)
-            at(normalise, step - 2, 1)
-            at(cell_tanh, step - 4)
-            at(multiply, step, 1, 0)
-            at(gate_sigmoid, step - 2, 0, 0)
+            at(multiply, step, 0, 1)
+            at(gate_sigmoid, step - 2, 0, 1)
             at(deviations, step, 0, 0)
-            at(new_hidden, step - 4, 0)
+            at(new_hidden, step - 4, 1)
+            at(transpose_operand, step + 2, 0, 1)
+            at(mean_and_inverse_std, step - 1)
+            at(normalise, step - 1, 1)
+            at(multiply, step, 1, 0)
+            at(gate_sigmoid, step - 2, 1, 0)
+            at(deviations, step, 0, 1)
+            at(keep_cell, step - 2, 0)
+            at(normalise, step - 1, 0)
             at(transpose_operand, step + 2, 1, 0)
             at(multiply, step, 1, 1)
-            at(gate_sigmoid, step - 2, 0, 1)
-            at(deviations, step, 0, 1)
-            at(new_hidden, step - 4, 1)
+            at(gate_sigmoid, step - 2, 1, 1)
+            at(deviations, step, 1, 0)
+            at(keep_cell, step - 2, 1)
+            at(cell_tanh, step - 3)
             at(transpose_operand, step + 2, 1, 1)
-            at(inverse_std, step - 1)
-            at(normalise, step - 1, 0)
-            at(add_candidate, step - 3)
+            at(add_candidate, step - 2)
 
         load_weight(Wf_w)
         load_biases()
@@ -352,8 +353,8 @@ def tile_layernormlstmcell_pb_t_kernel(
         transpose_operand(0, 1, 1)
         prepare_weight(2)
         quantise_operands(0)
-        spread_biases()
         prepare_weight(3)
+        spread_biases()
         turn_affine()
-        for step in range(-1, GROUPS + 5):
+        for step in range(-1, GROUPS + 4):
             run_step(step)

@@ -160,7 +160,7 @@ def tile_layernormlstmcell_pb_t_kernel(
             grouped_words = live["grouped", g][:].bitcast(F32).rearrange(
                 "p (t o r u) -> p t o r u", t=TILES, o=2, u=2
             )
-            copy = nc.scalar.copy if t == 0 else nc.vector.tensor_copy
+            copy = nc.vector.tensor_copy
             copy(out=grouped_words[:, t], in_=turned[:].rearrange("p (o u) r -> p o r u", o=2))
 
         def quantise_operands(g):
@@ -226,19 +226,31 @@ def tile_layernormlstmcell_pb_t_kernel(
             )
             nc.gpsimd.tensor_tensor(out=rstd[:], in0=var_eps[:], in1=neg_half[:], op=ALU.pow)
             live["rstd", g] = rstd
+            offset = stats.tile([P, TILES * GATES], F32, name="offset")
+            nc.gpsimd.tensor_tensor(out=offset[:], in0=neg_mean[:], in1=rstd[:], op=ALU.mult)
+            live["offset", g] = offset
 
         def normalise(g, gate):
             for t in range(TILES):
                 col = GATES * t + gate
                 act = live["act", g][:, gate, t, :]
-                (nc.vector if gate == 0 or g >= GROUPS - 1 else nc.gpsimd).tensor_scalar(
-                    out=act,
-                    in0=act,
-                    scalar1=live["neg_mean", g][:, col : col + 1],
-                    scalar2=live["rstd", g][:, col : col + 1],
-                    op0=ALU.add,
-                    op1=ALU.mult,
-                )
+                if gate == 0:
+                    nc.scalar.activation(
+                        out=act,
+                        in_=act,
+                        func=ACT.Identity,
+                        scale=live["rstd", g][:, col : col + 1],
+                        bias=live["offset", g][:, col : col + 1],
+                    )
+                else:
+                    (nc.vector if g >= GROUPS - 1 else nc.gpsimd).tensor_scalar(
+                        out=act,
+                        in0=act,
+                        scalar1=live["neg_mean", g][:, col : col + 1],
+                        scalar2=live["rstd", g][:, col : col + 1],
+                        op0=ALU.add,
+                        op1=ALU.mult,
+                    )
 
         def gate_sigmoid(g, gate, half):
             if half == 0:

@@ -21,6 +21,7 @@ TILES = 2
 GROUPS = BATCH // (P * TILES)
 GATES = 2
 EPS = 1e-5
+EARLY_GROUPS = 2
 
 FLOPS = 4 * 2 * BATCH * K * FEAT
 
@@ -82,7 +83,7 @@ def tile_layernormlstmcell_pb_t_kernel(
             grouped = wstage.tile([P, 4 * FEAT], BF16, name="w_grouped", align_bytes=64)
             grouped_words = grouped[:].bitcast(F32).rearrange("p (j u) -> p j u", u=2)
             for half in range(2):
-                turned = psum.tile([P, 2, 2 * P], F32, name="w_turned", tag=("turned", "norm", "back", "acc")[w])
+                turned = psum.tile([P, 2, 2 * P], F32, name="w_turned", tag=("turned", "norm", "back", "norm")[w])
                 for u in range(2):
                     for b in range(2):
                         first = (2 * half + b) * WORDS
@@ -105,7 +106,7 @@ def tile_layernormlstmcell_pb_t_kernel(
         bias = consts.tile([P, GATES * FEAT], BF16)
 
         def spread_biases():
-            bias_ps = psum.tile([P, GATES * FEAT], BF16, name="bias_ps", tag="norm")
+            bias_ps = psum.tile([P, GATES * FEAT], BF16, name="bias_ps", tag="back")
             for gate in range(GATES):
                 cols = slice(gate * FEAT, (gate + 1) * FEAT)
                 nc.tensor.matmul(out=bias_ps[:, cols], lhsT=ones[:], rhs=bias_rows[:, cols], start=True, stop=True)
@@ -160,7 +161,7 @@ def tile_layernormlstmcell_pb_t_kernel(
             grouped_words = live["grouped", g][:].bitcast(F32).rearrange(
                 "p (t o r u) -> p t o r u", t=TILES, o=2, u=2
             )
-            copy = nc.vector.tensor_copy
+            copy = nc.scalar.copy if g < EARLY_GROUPS else nc.vector.tensor_copy
             copy(out=grouped_words[:, t], in_=turned[:].rearrange("p (o u) r -> p o r u", o=2))
 
         def quantise_operands(g):
@@ -313,8 +314,11 @@ def tile_layernormlstmcell_pb_t_kernel(
             if t == TILES - 1:
                 nc.sync.dma_start(out=h_new_rows[g], in_=hidden[:].rearrange("p t f -> p (t f)"))
 
+        done = set()
+
         def at(stage, g, *args):
-            if 0 <= g < GROUPS:
+            if 0 <= g < GROUPS and (stage, g, args) not in done:
+                done.add((stage, g, args))
                 stage(g, *args)
 
         def run_step(step):
@@ -325,8 +329,7 @@ def tile_layernormlstmcell_pb_t_kernel(
             at(deviations, step - 1, 1, 1)
             at(new_hidden, step - 4, 0)
             at(transpose_operand, step + 2, 0, 0)
-            if step >= 0:
-                at(quantise_operands, step + 1)
+            at(quantise_operands, step + 1)
             at(multiply, step, 0, 1)
             at(gate_sigmoid, step - 2, 0, 1)
             at(deviations, step, 0, 0)
@@ -351,22 +354,23 @@ def tile_layernormlstmcell_pb_t_kernel(
         load_weight(Wf_w)
         load_biases()
         load_weight(Uf_w)
-        load_operands(0)
+        at(load_operands, 0)
         load_weight(Wo_w)
         load_weight(Uo_w)
         load_affine()
-        load_operands(1)
-        load_operands(2)
+        at(load_operands, 1)
+        at(load_operands, 2)
         prepare_weight(0)
-        prepare_weight(1)
-        transpose_operand(0, 0, 0)
-        transpose_operand(0, 0, 1)
-        transpose_operand(0, 1, 0)
-        transpose_operand(0, 1, 1)
-        prepare_weight(2)
-        quantise_operands(0)
-        prepare_weight(3)
         spread_biases()
+        prepare_weight(1)
+        for t in range(TILES):
+            for operand in range(2):
+                at(transpose_operand, 0, t, operand)
+        at(quantise_operands, 0)
+        prepare_weight(2)
+        at(multiply, 0, 0, 0)
+        at(multiply, 0, 1, 0)
+        prepare_weight(3)
         turn_affine()
         for step in range(-1, GROUPS + 4):
             run_step(step)

from contextlib import ExitStack

import concourse.mybir as mybir
from concourse.masks import make_identity

F32 = mybir.dt.float32
BF16 = mybir.dt.bfloat16
U32 = mybir.dt.uint32
U8 = mybir.dt.uint8
FP8X4 = mybir.dt.float8_e4m3fn_x4
ALU = mybir.AluOpType
ACT = mybir.ActivationFunctionType

P = 128
BATCH = 4096
K = 512
FEAT = 512
BLOCKS = FEAT // P
WORDS = K // 2
TILES = 2
GROUPS = BATCH // (P * TILES)
GATES = 2
EPS = 1e-5
EARLY_GROUPS = 2

FLOPS = 4 * 2 * BATCH * K * FEAT


def tile_layernormlstmcell_pb_t_kernel(
    tc, x, h, c, ic_tilde, Wf_w, Wf_b, Uf_w, lnf_g, lnf_b, Wo_w, Wo_b, Uo_w, lno_g, lno_b, out_0, out_1
):
    nc = tc.nc
    with ExitStack() as ctx:
        ctx.enter_context(tc.manual_schedule())
        consts = ctx.enter_context(tc.tile_pool(name="consts", bufs=1))
        wstage = ctx.enter_context(tc.tile_pool(name="wstage", bufs=2))
        loads = ctx.enter_context(tc.tile_pool(name="loads", bufs=4))
        mxin = ctx.enter_context(tc.tile_pool(name="mxin", bufs=3))
        stats = ctx.enter_context(tc.tile_pool(name="stats", bufs=5))
        acts = ctx.enter_context(tc.tile_pool(name="acts", bufs=5))
        scrap = ctx.enter_context(tc.tile_pool(name="scrap", bufs=2))
        psum = ctx.enter_context(tc.psum_pool(name="psum", bufs=2))

        ident = consts.tile([P, P], F32)
        make_identity(nc, ident[:])
        ident_bf16 = consts.tile([P, P], BF16)
        nc.vector.tensor_copy(out=ident_bf16[:], in_=ident[:])
        ones = consts.tile([P, P], BF16)
        nc.vector.memset(ones[:], 1.0)
        neg_half = consts.tile([P, TILES * GATES], F32)
        nc.vector.memset(neg_half[:], -0.5)
        bias_rows = consts.tile([P, GATES * FEAT], BF16)
        nc.vector.memset(bias_rows[:], 0.0)
        affine_rows = consts.tile([P, P], BF16)
        nc.vector.memset(affine_rows[:], 0.0)
        warm = consts.tile([P, 1], F32)
        nc.scalar.activation(out=warm[:], in_=neg_half[:, 0:1], func=ACT.Sigmoid)

        w_codes = consts.tile([P, 4 * FEAT], U32, align_bytes=64)
        w_scales = consts.tile([P, 4 * FEAT], U8, align_bytes=64)
        raws = []

        def load_weight(weight):
            raw = consts.tile([P, 4 * K], BF16, name="raw%d" % len(raws))
            nc.sync.dma_start(
                out=raw[:].rearrange("p (b k) -> p b k", b=4),
                in_=weight.rearrange("(b p) k -> p b k", p=P),
            )
            raws.append(raw)

        def load_biases():
            for v, vec in enumerate((Wf_b, Wo_b)):
                nc.sync.dma_start(out=bias_rows[0:1, v * FEAT : (v + 1) * FEAT], in_=vec.unsqueeze(0))

        def load_affine():
            for v, vec in enumerate((lnf_g, lnf_b, lno_g, lno_b)):
                nc.sync.dma_start(
                    out=affine_rows[BLOCKS * v : BLOCKS * (v + 1), :], in_=vec.rearrange("(j p) -> j p", p=P)
                )

        def prepare_weight(w):
            raw_words = raws[w][:].bitcast(F32)
            grouped = wstage.tile([P, 4 * FEAT], BF16, name="w_grouped", align_bytes=64)
            grouped_words = grouped[:].bitcast(F32).rearrange("p (j u) -> p j u", u=2)
            for half in range(2):
                turned = psum.tile([P, 2, 2 * P], F32, name="w_turned", tag=("turned", "norm", "back", "norm")[w])
                for u in range(2):
                    for b in range(2):
                        first = (2 * half + b) * WORDS
                        nc.tensor.transpose(
                            out=turned[:, u, b * P : (b + 1) * P],
                            in_=raw_words[:, first + u : first + WORDS : 2],
                            identity=ident[:],
                        )
                copy = nc.scalar.copy if half == 0 else nc.vector.tensor_copy
                copy(
                    out=grouped_words[:, half * 2 * P : (half + 1) * 2 * P, :],
                    in_=turned[:].rearrange("p u j -> p j u"),
                )
            nc.vector.quantize_mx(
                out=w_codes[:, w * FEAT : (w + 1) * FEAT].bitcast(FP8X4),
                scales=w_scales[:, w * FEAT : (w + 1) * FEAT],
                in_=grouped[:],
            )

        bias = consts.tile([P, GATES * FEAT], BF16)

        def spread_biases():
            bias_ps = psum.tile([P, GATES * FEAT], BF16, name="bias_ps", tag="back")
            for gate in range(GATES):
                cols = slice(gate * FEAT, (gate + 1) * FEAT)
                nc.tensor.matmul(out=bias_ps[:, cols], lhsT=ones[:], rhs=bias_rows[:, cols], start=True, stop=True)
            nc.scalar.copy(out=bias[:], in_=bias_ps[:])

        affine = consts.tile([P, 4 * BLOCKS], F32)

        def turn_affine():
            affine_ps = psum.tile([P, GATES * FEAT], BF16, name="affine_ps", tag="back")
            nc.tensor.transpose(out=affine_ps[:, 0:P], in_=affine_rows[:], identity=ident_bf16[:])
            nc.vector.tensor_copy(out=affine[:], in_=affine_ps[:, 0 : 4 * BLOCKS])

        rows = "(g p t) k -> g p (t k)"
        x_rows = x.rearrange(rows, p=P, t=TILES)
        h_rows = h.rearrange(rows, p=P, t=TILES)
        c_rows = c.rearrange(rows, p=P, t=TILES)
        ic_rows = ic_tilde.rearrange(rows, p=P, t=TILES)
        h_new_rows = out_0.rearrange(rows, p=P, t=TILES)
        c_new_rows = out_1.rearrange(rows, p=P, t=TILES)
        live = {}

        def load_operands(g):
            xh = loads.tile([P, 2 * TILES * K], BF16, name="xh")
            nc.sync.dma_start(out=xh[:, 0 : TILES * K], in_=x_rows[g])
            nc.sync.dma_start(out=xh[:, TILES * K : 2 * TILES * K], in_=h_rows[g])
            live["xh", g] = xh

        def load_cell(g):
            c_old = loads.tile([P, TILES, FEAT], BF16, name="c_old")
            ic = loads.tile([P, TILES, FEAT], BF16, name="ic")
            nc.sync.dma_start(out=c_old[:].rearrange("p t f -> p (t f)"), in_=c_rows[g])
            nc.sync.dma_start(out=ic[:].rearrange("p t f -> p (t f)"), in_=ic_rows[g])
            live["c_old", g] = c_old
            live["ic", g] = ic

        def transpose_operand(g, t, operand):
            words = live["xh", g][:].bitcast(F32)
            if operand == 0:
                live["turned", g, t] = psum.tile([P, 4, P], F32, name="turned", tag="turned")
            turned = live["turned", g, t]
            for u in range(2):
                first = (operand * TILES + t) * WORDS
                nc.tensor.transpose(
                    out=turned[:, 2 * operand + u, :],
                    in_=words[:, first + u : first + WORDS : 2],
                    identity=ident[:],
                )
            if operand == 0:
                return
            if t == 0:
                live["grouped", g] = mxin.tile([P, TILES * 2 * P * 4], BF16, name="grouped", align_bytes=64)
            grouped_words = live["grouped", g][:].bitcast(F32).rearrange(
                "p (t o r u) -> p t o r u", t=TILES, o=2, u=2
            )
            copy = nc.scalar.copy if g < EARLY_GROUPS else nc.vector.tensor_copy
            copy(out=grouped_words[:, t], in_=turned[:].rearrange("p (o u) r -> p o r u", o=2))

        def quantise_operands(g):
            codes = mxin.tile([P, TILES * 2 * P], U32, name="codes", align_bytes=64)
            scales = mxin.tile([P, TILES * 2 * P], U8, name="scales", align_bytes=64)
            nc.vector.quantize_mx(out=codes[:].bitcast(FP8X4), scales=scales[:], in_=live["grouped", g][:])
            live["codes", g] = codes
            live["scales", g] = scales

        def multiply(g, t, gate):
            codes, scales = live["codes", g], live["scales", g]
            if t == 0 and gate == 0:
                live["act", g] = acts.tile([P, GATES, TILES, FEAT], F32, name="act")
                live["sums", g] = stats.tile([P, TILES * GATES], F32, name="sums")
            acc = psum.tile([P, FEAT], F32, name="acc", tag="acc")
            for operand in range(2):
                r_cols = slice((2 * t + operand) * P, (2 * t + operand + 1) * P)
                w_cols = slice((2 * gate + operand) * FEAT, (2 * gate + operand + 1) * FEAT)
                nc.tensor.matmul_mx(
                    out=acc[:],
                    lhsT=codes[:, r_cols].bitcast(FP8X4),
                    lhsT_scale=scales[:, r_cols],
                    rhs=w_codes[:, w_cols].bitcast(FP8X4),
                    rhs_scale=w_scales[:, w_cols],
                    start=(operand == 0),
                    stop=(operand == 1),
                )
            col = GATES * t + gate
            nc.vector.scalar_tensor_tensor(
                out=live["act", g][:, gate, t, :],
                in0=acc[:],
                scalar=1.0,
                in1=bias[:, gate * FEAT : (gate + 1) * FEAT],
                op0=ALU.mult,
                op1=ALU.add,
                accum_out=live["sums", g][:, col : col + 1],
            )

        def deviations(g, t, gate):
            if t == 0 and gate == 0:
                live["sq_dev", g] = stats.tile([P, TILES * GATES], F32, name="sq_dev")
            col = GATES * t + gate
            squares = scrap.tile([P, FEAT], F32, name="squares")
            nc.scalar.activation(
                out=squares[:],
                in_=live["act", g][:, gate, t, :],
                func=ACT.Square,
                bias=live["sums", g][:, col : col + 1],
                scale=-1.0 * FEAT,
                accum_out=live["sq_dev", g][:, col : col + 1],
            )

        def mean_and_inverse_std(g):
            neg_mean = stats.tile([P, TILES * GATES], F32, name="neg_mean")
            nc.gpsimd.tensor_scalar(
                out=neg_mean[:], in0=live["sums", g][:], scalar1=-1.0 / FEAT, scalar2=0.0, op0=ALU.mult, op1=ALU.add
            )
            live["neg_mean", g] = neg_mean
            var_eps = stats.tile([P, TILES * GATES], F32, name="var_eps")
            rstd = stats.tile([P, TILES * GATES], F32, name="rstd")
            nc.gpsimd.tensor_scalar(
                out=var_eps[:], in0=live["sq_dev", g][:], scalar1=1.0 / FEAT**3, scalar2=EPS, op0=ALU.mult, op1=ALU.add
            )
            nc.gpsimd.tensor_tensor(out=rstd[:], in0=var_eps[:], in1=neg_half[:], op=ALU.pow)
            live["rstd", g] = rstd
            offset = stats.tile([P, TILES * GATES], F32, name="offset")
            nc.gpsimd.tensor_tensor(out=offset[:], in0=neg_mean[:], in1=rstd[:], op=ALU.mult)
            live["offset", g] = offset

        def normalise(g, gate):
            for t in range(TILES):
                col = GATES * t + gate
                act = live["act", g][:, gate, t, :]
                if gate == 0:
                    nc.scalar.activation(
                        out=act,
                        in_=act,
                        func=ACT.Identity,
                        scale=live["rstd", g][:, col : col + 1],
                        bias=live["offset", g][:, col : col + 1],
                    )
                else:
                    (nc.vector if g >= GROUPS - 1 else nc.gpsimd).tensor_scalar(
                        out=act,
                        in0=act,
                        scalar1=live["neg_mean", g][:, col : col + 1],
                        scalar2=live["rstd", g][:, col : col + 1],
                        op0=ALU.add,
                        op1=ALU.mult,
                    )

        def gate_sigmoid(g, gate, half):
            if half == 0:
                live["sig", g, gate] = acts.tile([P, BLOCKS, TILES, P], F32, name="sig%d" % gate)
            norm = psum.tile([P, 2, TILES, P], F32, name="norm", tag="norm")
            for b in range(2):
                block = 2 * half + b
                for t in range(TILES):
                    nc.tensor.transpose(
                        out=norm[:, b, t, :],
                        in_=live["act", g][:, gate, t, block * P : (block + 1) * P],
                        identity=ident[:],
                    )
            for b in range(2):
                block = 2 * half + b
                gain = 2 * gate * BLOCKS + block
                shift = gain + BLOCKS
                nc.scalar.activation(
                    out=live["sig", g, gate][:, block],
                    in_=norm[:, b],
                    func=ACT.Sigmoid,
                    scale=affine[:, gain : gain + 1],
                    bias=affine[:, shift : shift + 1],
                )

        def gate_back(g, gate, t):
            bank = psum.tile([P, BLOCKS, P], F32, name="back", tag="back")
            for block in range(BLOCKS):
                nc.tensor.transpose(
                    out=bank[:, block, :], in_=live["sig", g, gate][:, block, t, :], identity=ident[:]
                )
            return bank[:].rearrange("p b f -> p (b f)")

        def keep_cell(g, t):
            if t == 0:
                live["cell", g] = acts.tile([P, TILES, FEAT], F32, name="cell")
            cell = live["cell", g]
            nc.vector.tensor_tensor(
                out=cell[:, t, :], in0=gate_back(g, 0, t), in1=live["c_old", g][:, t, :], op=ALU.mult
            )

        def add_candidate(g):
            cell = live["cell", g]
            for t in range(TILES):
                (nc.vector if g >= GROUPS - 1 else nc.gpsimd).tensor_tensor(out=cell[:, t, :], in0=cell[:, t, :], in1=live["ic", g][:, t, :], op=ALU.add)
            nc.sync.dma_start(out=c_new_rows[g], in_=cell[:].rearrange("p t f -> p (t f)"))

        def cell_tanh(g):
            tanh_c = acts.tile([P, TILES, FEAT], F32, name="tanh_c")
            nc.scalar.activation(out=tanh_c[:], in_=live["cell", g][:], func=ACT.Tanh)
            live["tanh_c", g] = tanh_c

        def new_hidden(g, t):
            if t == 0:
                live["hidden", g] = acts.tile([P, TILES, FEAT], F32, name="hidden")
            hidden = live["hidden", g]
            nc.vector.tensor_tensor(
                out=hidden[:, t, :], in0=gate_back(g, 1, t), in1=live["tanh_c", g][:, t, :], op=ALU.mult
            )
            if t == TILES - 1:
                nc.sync.dma_start(out=h_new_rows[g], in_=hidden[:].rearrange("p t f -> p (t f)"))

        done = set()

        def at(stage, g, *args):
            if 0 <= g < GROUPS and (stage, g, args) not in done:
                done.add((stage, g, args))
                stage(g, *args)

        def run_step(step):
            at(load_operands, step + 4)
            at(load_cell, step - 1)
            at(multiply, step, 0, 0)
            at(gate_sigmoid, step - 2, 0, 0)
            at(deviations, step - 1, 1, 1)
            at(new_hidden, step - 4, 0)
            at(transpose_operand, step + 2, 0, 0)
            at(quantise_operands, step + 1)
            at(multiply, step, 0, 1)
            at(gate_sigmoid, step - 2, 0, 1)
            at(deviations, step, 0, 0)
            at(new_hidden, step - 4, 1)
            at(transpose_operand, step + 2, 0, 1)
            at(mean_and_inverse_std, step - 1)
            at(normalise, step - 1, 1)
            at(multiply, step, 1, 0)
            at(gate_sigmoid, step - 2, 1, 0)
            at(deviations, step, 0, 1)
            at(keep_cell, step - 2, 0)
            at(normalise, step - 1, 0)
            at(transpose_operand, step + 2, 1, 0)
            at(multiply, step, 1, 1)
            at(gate_sigmoid, step - 2, 1, 1)
            at(deviations, step, 1, 0)
            at(keep_cell, step - 2, 1)
            at(cell_tanh, step - 3)
            at(transpose_operand, step + 2, 1, 1)
            at(add_candidate, step - 2)

        load_weight(Wf_w)
        load_biases()
        load_weight(Uf_w)
        at(load_operands, 0)
        load_weight(Wo_w)
        load_weight(Uo_w)
        load_affine()
        at(load_operands, 1)
        at(load_operands, 2)
        prepare_weight(0)
        spread_biases()
        prepare_weight(1)
        for t in range(TILES):
            for operand in range(2):
                at(transpose_operand, 0, t, operand)
        at(quantise_operands, 0)
        prepare_weight(2)
        at(multiply, 0, 0, 0)
        at(multiply, 0, 1, 0)
        prepare_weight(3)
        turn_affine()
        for step in range(-1, GROUPS + 4):
            run_step(step)
